import numpy as np
import ml_dtypes

BF16 = ml_dtypes.bfloat16


def bf(x):
    return np.asarray(x, np.float32).astype(BF16)


def f32(x):
    return np.asarray(x, np.float32)


def f64(x):
    return np.asarray(x).astype(np.float64)


def striped(idx):
    return np.tile(idx.reshape(-1, 16).T, (8, 1))


C, S, N, D = 512, 2048, 512, 128
SLOPE = 0.2


def setup_inputs():
    return {"adj": f32(np.random.random((C, S)) < 0.5), "s_src": f32(np.random.standard_normal((C, 1))), "s_dst": f32(np.random.standard_normal((1, N))), "hw": bf(3.0 * np.random.standard_normal((N, D))), "b": f32(0.1 * np.random.standard_normal((1, D))), "offs": striped(np.random.permutation(S)[:N])}


def reference(adj, s_src, s_dst, hw, b, offs):
    idx = offs[:16].T.reshape(-1)
    v = f64(s_src) + f64(s_dst)
    e = np.exp(np.maximum(v, SLOPE * v))
    p = f64(adj)[:, idx] * e
    z = p.sum(axis=1, keepdims=True)
    r = (p @ f64(hw)) / z + f64(b)
    return np.maximum(r, 0.0) + np.exp(np.minimum(r, 0.0)) - 1.0

@@ -1,0 +1,106 @@
+import concourse.mybir as mybir
+from concourse.masks import make_identity
+
+F32, BF16, U16 = mybir.dt.float32, mybir.dt.bfloat16, mybir.dt.uint16
+ALU = mybir.AluOpType
+ACT = mybir.ActivationFunctionType
+
+P = 128
+C, S, N, D = 512, 2048, 512, 128
+SLOPE = 0.2
+BLOCKS = C // P
+CHUNKS = N // P
+PAD = 16
+
+FLOPS = 2 * C * N * D
+
+
+def tile_graphattentionlayer_kernel(tc, adj, s_src, s_dst, hw, b, offs, out):
+    nc = tc.nc
+    adj_blocks = adj.rearrange("(p n) s -> n p s", n=BLOCKS)
+    out_blocks = out.rearrange("(p n) d -> n p d", n=BLOCKS)
+
+    with (
+        tc.tile_pool(name="held", bufs=1) as held,
+        tc.tile_pool(name="work", bufs=2) as work,
+        tc.psum_pool(name="psum", bufs=2) as psum,
+    ):
+        offsets = held.tile([P, N // 16], U16, name="offsets")
+        nc.sync.dma_start(offsets[:], offs)
+        windows = [held.tile([P, S], F32, name=f"window{n}") for n in range(BLOCKS)]
+        for n in range(BLOCKS):
+            nc.sync.dma_start(windows[n][:], adj_blocks[n])
+
+        dst = held.tile([P, N], F32, name="dst")
+        nc.scalar.dma_start(dst[:], s_dst.squeeze(0).partition_broadcast(P))
+        src = held.tile([P, BLOCKS], F32, name="src")
+        nc.scalar.dma_start(src[:], s_src.rearrange("(p n) o -> p (n o)", n=BLOCKS))
+        bias = held.tile([P, D], F32, name="bias")
+        nc.scalar.dma_start(bias[:], b.squeeze(0).partition_broadcast(P))
+        hw_ones = held.tile([P, CHUNKS, D + PAD], BF16, name="hw_ones")
+        nc.gpsimd.memset(hw_ones[:, :, D:], 1.0)
+        nc.scalar.dma_start(hw_ones[:, :, :D], hw.rearrange("(k q) d -> q k d", q=P))
+
+        identity = held.tile([P, P], F32, name="identity")
+        make_identity(nc, identity[:])
+
+        dst_slope = held.tile([P, N], F32, name="dst_slope")
+        nc.scalar.mul(dst_slope[:], dst[:], SLOPE)
+        u_max = held.tile([P, 1], F32, name="u_max")
+        nc.vector.reduce_max(u_max[:], dst[:], axis=mybir.AxisListType.X)
+        u_max_slope = held.tile([P, 1], F32, name="u_max_slope")
+        nc.vector.tensor_scalar_mul(u_max_slope[:], u_max[:], SLOPE)
+        drop = held.tile([P, BLOCKS], F32, name="drop")
+        nc.vector.tensor_scalar_mul(drop[:], src[:], 1.0 - SLOPE)
+        w_max = held.tile([P, BLOCKS], F32, name="w_max")
+        nc.vector.tensor_scalar(
+            w_max[:], drop[:], -1.0, u_max_slope[:, 0:1], op0=ALU.mult, op1=ALU.add
+        )
+        nc.vector.tensor_scalar_max(w_max[:], w_max[:], u_max[:, 0:1])
+        neg_w_max = held.tile([P, BLOCKS], F32, name="neg_w_max")
+        nc.vector.tensor_scalar_mul(neg_w_max[:], w_max[:], -1.0)
+
+        for n in range(BLOCKS):
+            w = work.tile([P, N], F32, name="w")
+            nc.vector.scalar_tensor_tensor(
+                w[:], dst_slope[:], drop[:, n : n + 1], dst[:], op0=ALU.subtract, op1=ALU.max
+            )
+            weight = work.tile([P, N], F32, name="weight")
+            nc.scalar.activation(weight[:], w[:], ACT.Exp, bias=neg_w_max[:, n : n + 1])
+
+            p = work.tile([P, N], F32, name="p")
+            nc.vector.tensor_tensor(p[:], windows[n][:].indirect(offsets[:]), weight[:], ALU.mult)
+
+            p_turned = psum.tile([P, N], F32, name="p_turned")
+            for k in range(CHUNKS):
+                nc.tensor.transpose(
+                    p_turned[:, k * P : (k + 1) * P], p[:, k * P : (k + 1) * P], identity[:]
+                )
+            p_bf = work.tile([P, N], BF16, name="p_bf")
+            nc.scalar.copy(p_bf[:], p_turned[:])
+
+            sums = psum.tile([P, D + 1], F32, name="sums")
+            for k in range(CHUNKS):
+                nc.tensor.matmul(
+                    sums[:],
+                    lhsT=p_bf[:, k * P : (k + 1) * P],
+                    rhs=hw_ones[:, k, : D + 1],
+                    start=(k == 0),
+                    stop=(k == CHUNKS - 1),
+                )
+
+            z_inv = work.tile([P, 1], F32, name="z_inv")
+            nc.vector.reciprocal(z_inv[:], sums[:, D : D + 1])
+            r = work.tile([P, D], F32, name="r")
+            nc.vector.scalar_tensor_tensor(
+                r[:], sums[:, :D], z_inv[:, 0:1], bias[:], op0=ALU.mult, op1=ALU.add
+            )
+            r_neg = work.tile([P, D], F32, name="r_neg")
+            nc.vector.tensor_scalar_min(r_neg[:], r[:], 0.0)
+            r_exp = work.tile([P, D], F32, name="r_exp")
+            nc.scalar.activation(r_exp[:], r_neg[:], ACT.Exp)
+            result = work.tile([P, D], F32, name="result")
+            nc.vector.scalar_tensor_tensor(
+                result[:], r_exp[:], -1.0, r[:], op0=ALU.add, op1=ALU.max
+            )
+            nc.sync.dma_start(out_blocks[n], result[:])

@@ -9,7 +9,9 @@ P = 128
 C, S, N, D = 512, 2048, 512, 128
 SLOPE = 0.2
 BLOCKS = C // P
-CHUNKS = N // P
+PIECE = 256
+PIECES = N // PIECE
+CHUNKS = PIECE // P
 PAD = 16
 
 FLOPS = 2 * C * N * D
@@ -22,72 +24,73 @@ def tile_graphattentionlayer_kernel(tc, adj, s_src, s_dst, hw, b, offs, out):
 
     with (
         tc.tile_pool(name="held", bufs=1) as held,
-        tc.tile_pool(name="work", bufs=2) as work,
-        tc.psum_pool(name="psum", bufs=2) as psum,
+        tc.tile_pool(name="work", bufs=3) as work,
+        tc.psum_pool(name="turned", bufs=4) as turned,
+        tc.psum_pool(name="summed", bufs=2) as summed,
     ):
         offsets = held.tile([P, N // 16], U16, name="offsets")
         nc.sync.dma_start(offsets[:], offs)
+        dst = held.tile([P, N], F32, name="dst")
+        nc.sync.dma_start(dst[:], s_dst.squeeze(0).partition_broadcast(P))
+        src = held.tile([P, BLOCKS], F32, name="src")
+        nc.sync.dma_start(src[:], s_src.rearrange("(p n) o -> p (n o)", n=BLOCKS))
         windows = [held.tile([P, S], F32, name=f"window{n}") for n in range(BLOCKS)]
         for n in range(BLOCKS):
             nc.sync.dma_start(windows[n][:], adj_blocks[n])
 
-        dst = held.tile([P, N], F32, name="dst")
-        nc.scalar.dma_start(dst[:], s_dst.squeeze(0).partition_broadcast(P))
-        src = held.tile([P, BLOCKS], F32, name="src")
-        nc.scalar.dma_start(src[:], s_src.rearrange("(p n) o -> p (n o)", n=BLOCKS))
-        bias = held.tile([P, D], F32, name="bias")
-        nc.scalar.dma_start(bias[:], b.squeeze(0).partition_broadcast(P))
-        hw_ones = held.tile([P, CHUNKS, D + PAD], BF16, name="hw_ones")
+        hw_ones = held.tile([P, N // P, D + PAD], BF16, name="hw_ones")
         nc.gpsimd.memset(hw_ones[:, :, D:], 1.0)
         nc.scalar.dma_start(hw_ones[:, :, :D], hw.rearrange("(k q) d -> q k d", q=P))
+        bias = held.tile([P, D], F32, name="bias")
+        nc.scalar.dma_start(bias[:], b.squeeze(0).partition_broadcast(P))
 
         identity = held.tile([P, P], F32, name="identity")
         make_identity(nc, identity[:])
 
         dst_slope = held.tile([P, N], F32, name="dst_slope")
         nc.scalar.mul(dst_slope[:], dst[:], SLOPE)
-        u_max = held.tile([P, 1], F32, name="u_max")
-        nc.vector.reduce_max(u_max[:], dst[:], axis=mybir.AxisListType.X)
-        u_max_slope = held.tile([P, 1], F32, name="u_max_slope")
-        nc.vector.tensor_scalar_mul(u_max_slope[:], u_max[:], SLOPE)
         drop = held.tile([P, BLOCKS], F32, name="drop")
         nc.vector.tensor_scalar_mul(drop[:], src[:], 1.0 - SLOPE)
-        w_max = held.tile([P, BLOCKS], F32, name="w_max")
-        nc.vector.tensor_scalar(
-            w_max[:], drop[:], -1.0, u_max_slope[:, 0:1], op0=ALU.mult, op1=ALU.add
-        )
-        nc.vector.tensor_scalar_max(w_max[:], w_max[:], u_max[:, 0:1])
+        u_max = held.tile([P, 1], F32, name="u_max")
+        nc.vector.reduce_max(u_max[:], dst[:], axis=mybir.AxisListType.X)
         neg_w_max = held.tile([P, BLOCKS], F32, name="neg_w_max")
-        nc.vector.tensor_scalar_mul(neg_w_max[:], w_max[:], -1.0)
-
+        nc.vector.tensor_scalar(neg_w_max[:], src[:], u_max[:, 0:1], 0.0, op0=ALU.add, op1=ALU.min)
+        nc.vector.tensor_scalar(
+            neg_w_max[:], neg_w_max[:], 1.0 - SLOPE, u_max[:, 0:1], op0=ALU.mult, op1=ALU.subtract
+        )
+        weights = [held.tile([P, N], F32, name=f"weight{n}") for n in range(BLOCKS)]
         for n in range(BLOCKS):
             w = work.tile([P, N], F32, name="w")
             nc.vector.scalar_tensor_tensor(
                 w[:], dst_slope[:], drop[:, n : n + 1], dst[:], op0=ALU.subtract, op1=ALU.max
             )
-            weight = work.tile([P, N], F32, name="weight")
-            nc.scalar.activation(weight[:], w[:], ACT.Exp, bias=neg_w_max[:, n : n + 1])
+            nc.scalar.activation(weights[n][:], w[:], ACT.Exp, bias=neg_w_max[:, n : n + 1])
 
-            p = work.tile([P, N], F32, name="p")
-            nc.vector.tensor_tensor(p[:], windows[n][:].indirect(offsets[:]), weight[:], ALU.mult)
-
-            p_turned = psum.tile([P, N], F32, name="p_turned")
-            for k in range(CHUNKS):
-                nc.tensor.transpose(
-                    p_turned[:, k * P : (k + 1) * P], p[:, k * P : (k + 1) * P], identity[:]
+        for n in range(BLOCKS):
+            sums = summed.tile([P, D + 1], F32, name="sums")
+            for i in range(PIECES):
+                p = work.tile([P, PIECE], F32, name="p")
+                nc.vector.tensor_tensor(
+                    p[:],
+                    windows[n][:].indirect(offsets[:, i * (PIECE // 16) : (i + 1) * (PIECE // 16)]),
+                    weights[n][:, i * PIECE : (i + 1) * PIECE],
+                    ALU.mult,
                 )
-            p_bf = work.tile([P, N], BF16, name="p_bf")
-            nc.scalar.copy(p_bf[:], p_turned[:])
-
-            sums = psum.tile([P, D + 1], F32, name="sums")
-            for k in range(CHUNKS):
-                nc.tensor.matmul(
-                    sums[:],
-                    lhsT=p_bf[:, k * P : (k + 1) * P],
-                    rhs=hw_ones[:, k, : D + 1],
-                    start=(k == 0),
-                    stop=(k == CHUNKS - 1),
-                )
+                p_turned = turned.tile([P, PIECE], F32, name="p_turned")
+                for k in range(CHUNKS):
+                    nc.tensor.transpose(
+                        p_turned[:, k * P : (k + 1) * P], p[:, k * P : (k + 1) * P], identity[:]
+                    )
+                p_bf = work.tile([P, PIECE], BF16, name="p_bf")
+                nc.scalar.copy(p_bf[:], p_turned[:])
+                for k in range(CHUNKS):
+                    nc.tensor.matmul(
+                        sums[:],
+                        lhsT=p_bf[:, k * P : (k + 1) * P],
+                        rhs=hw_ones[:, i * CHUNKS + k, : D + 1],
+                        start=(i == 0 and k == 0),
+                        stop=(i == PIECES - 1 and k == CHUNKS - 1),
+                    )
 
             z_inv = work.tile([P, 1], F32, name="z_inv")
             nc.vector.reciprocal(z_inv[:], sums[:, D : D + 1])
@@ -95,12 +98,12 @@ def tile_graphattentionlayer_kernel(tc, adj, s_src, s_dst, hw, b, offs, out):
             nc.vector.scalar_tensor_tensor(
                 r[:], sums[:, :D], z_inv[:, 0:1], bias[:], op0=ALU.mult, op1=ALU.add
             )
-            r_neg = work.tile([P, D], F32, name="r_neg")
-            nc.vector.tensor_scalar_min(r_neg[:], r[:], 0.0)
             r_exp = work.tile([P, D], F32, name="r_exp")
-            nc.scalar.activation(r_exp[:], r_neg[:], ACT.Exp)
+            nc.scalar.activation(r_exp[:], r[:], ACT.Exp)
+            r_pos = work.tile([P, D], F32, name="r_pos")
+            nc.vector.tensor_scalar_max(r_pos[:], r[:], 0.0)
             result = work.tile([P, D], F32, name="result")
             nc.vector.scalar_tensor_tensor(
-                result[:], r_exp[:], -1.0, r[:], op0=ALU.add, op1=ALU.max
+                result[:], r_exp[:], -1.0, r_pos[:], op0=ALU.add, op1=ALU.min
             )
             nc.sync.dma_start(out_blocks[n], result[:])

@@ -9,9 +9,7 @@ P = 128
 C, S, N, D = 512, 2048, 512, 128
 SLOPE = 0.2
 BLOCKS = C // P
-PIECE = 256
-PIECES = N // PIECE
-CHUNKS = PIECE // P
+CHUNKS = N // P
 PAD = 16
 
 FLOPS = 2 * C * N * D
@@ -24,25 +22,26 @@ def tile_graphattentionlayer_kernel(tc, adj, s_src, s_dst, hw, b, offs, out):
 
     with (
         tc.tile_pool(name="held", bufs=1) as held,
-        tc.tile_pool(name="work", bufs=3) as work,
-        tc.psum_pool(name="turned", bufs=4) as turned,
-        tc.psum_pool(name="summed", bufs=2) as summed,
+        tc.tile_pool(name="work", bufs=2) as work,
+        tc.tile_pool(name="last", bufs=BLOCKS) as last,
+        tc.psum_pool(name="turned", bufs=2) as turned,
+        tc.psum_pool(name="summed", bufs=BLOCKS) as summed,
     ):
         offsets = held.tile([P, N // 16], U16, name="offsets")
         nc.sync.dma_start(offsets[:], offs)
-        dst = held.tile([P, N], F32, name="dst")
-        nc.sync.dma_start(dst[:], s_dst.squeeze(0).partition_broadcast(P))
-        src = held.tile([P, BLOCKS], F32, name="src")
-        nc.sync.dma_start(src[:], s_src.rearrange("(p n) o -> p (n o)", n=BLOCKS))
         windows = [held.tile([P, S], F32, name=f"window{n}") for n in range(BLOCKS)]
         for n in range(BLOCKS):
             nc.sync.dma_start(windows[n][:], adj_blocks[n])
+        bias = held.tile([P, D], F32, name="bias")
+        nc.sync.dma_start(bias[:], b.squeeze(0).partition_broadcast(P))
 
-        hw_ones = held.tile([P, N // P, D + PAD], BF16, name="hw_ones")
+        dst = held.tile([P, N], F32, name="dst")
+        nc.scalar.dma_start(dst[:], s_dst.squeeze(0).partition_broadcast(P))
+        src = held.tile([P, BLOCKS], F32, name="src")
+        nc.scalar.dma_start(src[:], s_src.rearrange("(p n) o -> p (n o)", n=BLOCKS))
+        hw_ones = held.tile([P, CHUNKS, D + PAD], BF16, name="hw_ones")
         nc.gpsimd.memset(hw_ones[:, :, D:], 1.0)
         nc.scalar.dma_start(hw_ones[:, :, :D], hw.rearrange("(k q) d -> q k d", q=P))
-        bias = held.tile([P, D], F32, name="bias")
-        nc.scalar.dma_start(bias[:], b.squeeze(0).partition_broadcast(P))
 
         identity = held.tile([P, P], F32, name="identity")
         make_identity(nc, identity[:])
@@ -67,42 +66,38 @@ def tile_graphattentionlayer_kernel(tc, adj, s_src, s_dst, hw, b, offs, out):
             nc.scalar.activation(weights[n][:], w[:], ACT.Exp, bias=neg_w_max[:, n : n + 1])
 
         for n in range(BLOCKS):
-            sums = summed.tile([P, D + 1], F32, name="sums")
-            for i in range(PIECES):
-                p = work.tile([P, PIECE], F32, name="p")
-                nc.vector.tensor_tensor(
-                    p[:],
-                    windows[n][:].indirect(offsets[:, i * (PIECE // 16) : (i + 1) * (PIECE // 16)]),
-                    weights[n][:, i * PIECE : (i + 1) * PIECE],
-                    ALU.mult,
+            p = work.tile([P, N], F32, name="p")
+            nc.vector.tensor_tensor(
+                p[:], windows[n][:].indirect(offsets[:]), weights[n][:], ALU.mult
+            )
+            p_turned = turned.tile([P, N], F32, name="p_turned")
+            for k in range(CHUNKS):
+                nc.tensor.transpose(
+                    p_turned[:, k * P : (k + 1) * P], p[:, k * P : (k + 1) * P], identity[:]
                 )
-                p_turned = turned.tile([P, PIECE], F32, name="p_turned")
-                for k in range(CHUNKS):
-                    nc.tensor.transpose(
-                        p_turned[:, k * P : (k + 1) * P], p[:, k * P : (k + 1) * P], identity[:]
-                    )
-                p_bf = work.tile([P, PIECE], BF16, name="p_bf")
-                nc.scalar.copy(p_bf[:], p_turned[:])
-                for k in range(CHUNKS):
-                    nc.tensor.matmul(
-                        sums[:],
-                        lhsT=p_bf[:, k * P : (k + 1) * P],
-                        rhs=hw_ones[:, i * CHUNKS + k, : D + 1],
-                        start=(i == 0 and k == 0),
-                        stop=(i == PIECES - 1 and k == CHUNKS - 1),
-                    )
+            p_bf = work.tile([P, N], BF16, name="p_bf")
+            nc.scalar.copy(p_bf[:], p_turned[:])
+            sums = summed.tile([P, D + 1], F32, name="sums")
+            for k in range(CHUNKS):
+                nc.tensor.matmul(
+                    sums[:],
+                    lhsT=p_bf[:, k * P : (k + 1) * P],
+                    rhs=hw_ones[:, k, : D + 1],
+                    start=(k == 0),
+                    stop=(k == CHUNKS - 1),
+                )
 
-            z_inv = work.tile([P, 1], F32, name="z_inv")
+            z_inv = last.tile([P, 1], F32, name="z_inv")
             nc.vector.reciprocal(z_inv[:], sums[:, D : D + 1])
-            r = work.tile([P, D], F32, name="r")
+            r = last.tile([P, D], F32, name="r")
             nc.vector.scalar_tensor_tensor(
                 r[:], sums[:, :D], z_inv[:, 0:1], bias[:], op0=ALU.mult, op1=ALU.add
             )
-            r_exp = work.tile([P, D], F32, name="r_exp")
+            r_exp = last.tile([P, D], F32, name="r_exp")
             nc.scalar.activation(r_exp[:], r[:], ACT.Exp)
-            r_pos = work.tile([P, D], F32, name="r_pos")
+            r_pos = last.tile([P, D], F32, name="r_pos")
             nc.vector.tensor_scalar_max(r_pos[:], r[:], 0.0)
-            result = work.tile([P, D], F32, name="result")
+            result = last.tile([P, D], F32, name="result")
             nc.vector.scalar_tensor_tensor(
                 result[:], r_exp[:], -1.0, r_pos[:], op0=ALU.add, op1=ALU.min
             )

@@ -22,10 +22,9 @@ def tile_graphattentionlayer_kernel(tc, adj, s_src, s_dst, hw, b, offs, out):
 
     with (
         tc.tile_pool(name="held", bufs=1) as held,
-        tc.tile_pool(name="work", bufs=2) as work,
-        tc.tile_pool(name="last", bufs=BLOCKS) as last,
-        tc.psum_pool(name="turned", bufs=2) as turned,
-        tc.psum_pool(name="summed", bufs=BLOCKS) as summed,
+        tc.tile_pool(name="work", bufs=4) as work,
+        tc.psum_pool(name="turned", bufs=4) as turned,
+        tc.psum_pool(name="summed", bufs=1) as summed,
     ):
         offsets = held.tile([P, N // 16], U16, name="offsets")
         nc.sync.dma_start(offsets[:], offs)
@@ -65,39 +64,40 @@ def tile_graphattentionlayer_kernel(tc, adj, s_src, s_dst, hw, b, offs, out):
             )
             nc.scalar.activation(weights[n][:], w[:], ACT.Exp, bias=neg_w_max[:, n : n + 1])
 
+        sums = [summed.tile([P, D + 1], F32, name=f"sums{n}") for n in range(BLOCKS)]
         for n in range(BLOCKS):
-            p = work.tile([P, N], F32, name="p")
-            nc.vector.tensor_tensor(
-                p[:], windows[n][:].indirect(offsets[:]), weights[n][:], ALU.mult
-            )
-            p_turned = turned.tile([P, N], F32, name="p_turned")
             for k in range(CHUNKS):
-                nc.tensor.transpose(
-                    p_turned[:, k * P : (k + 1) * P], p[:, k * P : (k + 1) * P], identity[:]
+                p = work.tile([P, P], F32, name="p")
+                nc.vector.tensor_tensor(
+                    p[:],
+                    windows[n][:].indirect(offsets[:, k * (P // 16) : (k + 1) * (P // 16)]),
+                    weights[n][:, k * P : (k + 1) * P],
+                    ALU.mult,
                 )
-            p_bf = work.tile([P, N], BF16, name="p_bf")
-            nc.scalar.copy(p_bf[:], p_turned[:])
-            sums = summed.tile([P, D + 1], F32, name="sums")
-            for k in range(CHUNKS):
+                p_turned = turned.tile([P, P], F32, name="p_turned")
+                nc.tensor.transpose(p_turned[:], p[:], identity[:])
+                p_bf = work.tile([P, P], BF16, name="p_bf")
+                nc.scalar.copy(p_bf[:], p_turned[:])
                 nc.tensor.matmul(
-                    sums[:],
-                    lhsT=p_bf[:, k * P : (k + 1) * P],
+                    sums[n][:],
+                    lhsT=p_bf[:],
                     rhs=hw_ones[:, k, : D + 1],
                     start=(k == 0),
                     stop=(k == CHUNKS - 1),
                 )
 
-            z_inv = last.tile([P, 1], F32, name="z_inv")
-            nc.vector.reciprocal(z_inv[:], sums[:, D : D + 1])
-            r = last.tile([P, D], F32, name="r")
+        for n in range(BLOCKS):
+            z_inv = work.tile([P, 1], F32, name="z_inv")
+            nc.vector.reciprocal(z_inv[:], sums[n][:, D : D + 1])
+            r = work.tile([P, D], F32, name="r")
             nc.vector.scalar_tensor_tensor(
-                r[:], sums[:, :D], z_inv[:, 0:1], bias[:], op0=ALU.mult, op1=ALU.add
+                r[:], sums[n][:, :D], z_inv[:, 0:1], bias[:], op0=ALU.mult, op1=ALU.add
             )
-            r_exp = last.tile([P, D], F32, name="r_exp")
+            r_exp = work.tile([P, D], F32, name="r_exp")
             nc.scalar.activation(r_exp[:], r[:], ACT.Exp)
-            r_pos = last.tile([P, D], F32, name="r_pos")
+            r_pos = work.tile([P, D], F32, name="r_pos")
             nc.vector.tensor_scalar_max(r_pos[:], r[:], 0.0)
-            result = last.tile([P, D], F32, name="result")
+            result = work.tile([P, D], F32, name="result")
             nc.vector.scalar_tensor_tensor(
                 result[:], r_exp[:], -1.0, r_pos[:], op0=ALU.add, op1=ALU.min
             )

@@ -26,6 +26,8 @@ def tile_graphattentionlayer_kernel(tc, adj, s_src, s_dst, hw, b, offs, out):
         tc.psum_pool(name="turned", bufs=4) as turned,
         tc.psum_pool(name="summed", bufs=1) as summed,
     ):
+        dst = held.tile([P, N], F32, name="dst")
+        nc.sync.dma_start(dst[:], s_dst.squeeze(0).partition_broadcast(P))
         offsets = held.tile([P, N // 16], U16, name="offsets")
         nc.sync.dma_start(offsets[:], offs)
         windows = [held.tile([P, S], F32, name=f"window{n}") for n in range(BLOCKS)]
@@ -34,8 +36,6 @@ def tile_graphattentionlayer_kernel(tc, adj, s_src, s_dst, hw, b, offs, out):
         bias = held.tile([P, D], F32, name="bias")
         nc.sync.dma_start(bias[:], b.squeeze(0).partition_broadcast(P))
 
-        dst = held.tile([P, N], F32, name="dst")
-        nc.scalar.dma_start(dst[:], s_dst.squeeze(0).partition_broadcast(P))
         src = held.tile([P, BLOCKS], F32, name="src")
         nc.scalar.dma_start(src[:], s_src.rearrange("(p n) o -> p (n o)", n=BLOCKS))
         hw_ones = held.tile([P, CHUNKS, D + PAD], BF16, name="hw_ones")
@@ -96,7 +96,7 @@ def tile_graphattentionlayer_kernel(tc, adj, s_src, s_dst, hw, b, offs, out):
             r_exp = work.tile([P, D], F32, name="r_exp")
             nc.scalar.activation(r_exp[:], r[:], ACT.Exp)
             r_pos = work.tile([P, D], F32, name="r_pos")
-            nc.vector.tensor_scalar_max(r_pos[:], r[:], 0.0)
+            nc.gpsimd.tensor_scalar_max(r_pos[:], r[:], 0.0)
             result = work.tile([P, D], F32, name="result")
             nc.vector.scalar_tensor_tensor(
                 result[:], r_exp[:], -1.0, r_pos[:], op0=ALU.add, op1=ALU.min

@@ -66,25 +66,28 @@ def tile_graphattentionlayer_kernel(tc, adj, s_src, s_dst, hw, b, offs, out):
 
         sums = [summed.tile([P, D + 1], F32, name=f"sums{n}") for n in range(BLOCKS)]
         for n in range(BLOCKS):
-            for k in range(CHUNKS):
-                p = work.tile([P, P], F32, name="p")
+            piece = P if n == BLOCKS - 1 else N
+            for first in range(0, N, piece):
+                p = work.tile([P, piece], F32, name=f"p{piece}")
                 nc.vector.tensor_tensor(
                     p[:],
-                    windows[n][:].indirect(offsets[:, k * (P // 16) : (k + 1) * (P // 16)]),
-                    weights[n][:, k * P : (k + 1) * P],
+                    windows[n][:].indirect(offsets[:, first // 16 : (first + piece) // 16]),
+                    weights[n][:, first : first + piece],
                     ALU.mult,
                 )
-                p_turned = turned.tile([P, P], F32, name="p_turned")
-                nc.tensor.transpose(p_turned[:], p[:], identity[:])
-                p_bf = work.tile([P, P], BF16, name="p_bf")
+                p_turned = turned.tile([P, piece], F32, name="p_turned")
+                for at in range(0, piece, P):
+                    nc.tensor.transpose(p_turned[:, at : at + P], p[:, at : at + P], identity[:])
+                p_bf = work.tile([P, piece], BF16, name=f"p_bf{piece}")
                 nc.scalar.copy(p_bf[:], p_turned[:])
-                nc.tensor.matmul(
-                    sums[n][:],
-                    lhsT=p_bf[:],
-                    rhs=hw_ones[:, k, : D + 1],
-                    start=(k == 0),
-                    stop=(k == CHUNKS - 1),
-                )
+                for at in range(0, piece, P):
+                    nc.tensor.matmul(
+                        sums[n][:],
+                        lhsT=p_bf[:, at : at + P],
+                        rhs=hw_ones[:, (first + at) // P, : D + 1],
+                        start=(first + at == 0),
+                        stop=(first + at == N - P),
+                    )
 
         for n in range(BLOCKS):
             z_inv = work.tile([P, 1], F32, name="z_inv")
@@ -96,7 +99,7 @@ def tile_graphattentionlayer_kernel(tc, adj, s_src, s_dst, hw, b, offs, out):
             r_exp = work.tile([P, D], F32, name="r_exp")
             nc.scalar.activation(r_exp[:], r[:], ACT.Exp)
             r_pos = work.tile([P, D], F32, name="r_pos")
-            nc.gpsimd.tensor_scalar_max(r_pos[:], r[:], 0.0)
+            nc.vector.tensor_scalar_max(r_pos[:], r[:], 0.0)
             result = work.tile([P, D], F32, name="result")
             nc.vector.scalar_tensor_tensor(
                 result[:], r_exp[:], -1.0, r_pos[:], op0=ALU.add, op1=ALU.min

@@ -90,16 +90,17 @@ def tile_graphattentionlayer_kernel(tc, adj, s_src, s_dst, hw, b, offs, out):
                     )
 
         for n in range(BLOCKS):
+            z = sums[n][:, D : D + 1]
             z_inv = work.tile([P, 1], F32, name="z_inv")
-            nc.vector.reciprocal(z_inv[:], sums[n][:, D : D + 1])
-            r = work.tile([P, D], F32, name="r")
+            nc.vector.reciprocal(z_inv[:], z)
+            r_z = work.tile([P, D], F32, name="r_z")
             nc.vector.scalar_tensor_tensor(
-                r[:], sums[n][:, :D], z_inv[:, 0:1], bias[:], op0=ALU.mult, op1=ALU.add
+                r_z[:], bias[:], z, sums[n][:, :D], op0=ALU.mult, op1=ALU.add
             )
             r_exp = work.tile([P, D], F32, name="r_exp")
-            nc.scalar.activation(r_exp[:], r[:], ACT.Exp)
+            nc.scalar.activation(r_exp[:], r_z[:], ACT.Exp, scale=z_inv[:, 0:1])
             r_pos = work.tile([P, D], F32, name="r_pos")
-            nc.vector.tensor_scalar_max(r_pos[:], r[:], 0.0)
+            nc.vector.tensor_scalar(r_pos[:], r_z[:], z_inv[:, 0:1], 0.0, op0=ALU.mult, op1=ALU.max)
             result = work.tile([P, D], F32, name="result")
             nc.vector.scalar_tensor_tensor(
                 result[:], r_exp[:], -1.0, r_pos[:], op0=ALU.add, op1=ALU.min

@@ -23,11 +23,14 @@ def tile_graphattentionlayer_kernel(tc, adj, s_src, s_dst, hw, b, offs, out):
     with (
         tc.tile_pool(name="held", bufs=1) as held,
         tc.tile_pool(name="work", bufs=4) as work,
+        tc.tile_pool(name="pair", bufs=2) as pair,
         tc.psum_pool(name="turned", bufs=4) as turned,
         tc.psum_pool(name="summed", bufs=1) as summed,
     ):
-        dst = held.tile([P, N], F32, name="dst")
-        nc.sync.dma_start(dst[:], s_dst.squeeze(0).partition_broadcast(P))
+        dst_columns = held.tile([P, CHUNKS], F32, name="dst_columns")
+        nc.sync.dma_start(dst_columns[:], s_dst.rearrange("o (q k) -> q (k o)", k=CHUNKS))
+        src = held.tile([P, BLOCKS], F32, name="src")
+        nc.sync.dma_start(src[:], s_src.rearrange("(p n) o -> p (n o)", n=BLOCKS))
         offsets = held.tile([P, N // 16], U16, name="offsets")
         nc.sync.dma_start(offsets[:], offs)
         windows = [held.tile([P, S], F32, name=f"window{n}") for n in range(BLOCKS)]
@@ -36,8 +39,6 @@ def tile_graphattentionlayer_kernel(tc, adj, s_src, s_dst, hw, b, offs, out):
         bias = held.tile([P, D], F32, name="bias")
         nc.sync.dma_start(bias[:], b.squeeze(0).partition_broadcast(P))
 
-        src = held.tile([P, BLOCKS], F32, name="src")
-        nc.scalar.dma_start(src[:], s_src.rearrange("(p n) o -> p (n o)", n=BLOCKS))
         hw_ones = held.tile([P, CHUNKS, D + PAD], BF16, name="hw_ones")
         nc.gpsimd.memset(hw_ones[:, :, D:], 1.0)
         nc.scalar.dma_start(hw_ones[:, :, :D], hw.rearrange("(k q) d -> q k d", q=P))
@@ -45,37 +46,65 @@ def tile_graphattentionlayer_kernel(tc, adj, s_src, s_dst, hw, b, offs, out):
         identity = held.tile([P, P], F32, name="identity")
         make_identity(nc, identity[:])
 
-        dst_slope = held.tile([P, N], F32, name="dst_slope")
-        nc.scalar.mul(dst_slope[:], dst[:], SLOPE)
-        drop = held.tile([P, BLOCKS], F32, name="drop")
-        nc.vector.tensor_scalar_mul(drop[:], src[:], 1.0 - SLOPE)
-        u_max = held.tile([P, 1], F32, name="u_max")
-        nc.vector.reduce_max(u_max[:], dst[:], axis=mybir.AxisListType.X)
-        neg_w_max = held.tile([P, BLOCKS], F32, name="neg_w_max")
-        nc.vector.tensor_scalar(neg_w_max[:], src[:], u_max[:, 0:1], 0.0, op0=ALU.add, op1=ALU.min)
-        nc.vector.tensor_scalar(
-            neg_w_max[:], neg_w_max[:], 1.0 - SLOPE, u_max[:, 0:1], op0=ALU.mult, op1=ALU.subtract
-        )
-        weights = [held.tile([P, N], F32, name=f"weight{n}") for n in range(BLOCKS)]
-        for n in range(BLOCKS):
-            w = work.tile([P, N], F32, name="w")
-            nc.vector.scalar_tensor_tensor(
-                w[:], dst_slope[:], drop[:, n : n + 1], dst[:], op0=ALU.subtract, op1=ALU.max
+        dst_peaks = held.tile([P, 1], F32, name="dst_peaks")
+        nc.vector.reduce_max(dst_peaks[:], dst_columns[:], axis=mybir.AxisListType.X)
+
+        peaks = turned.tile([P, P], F32, name="peaks", tag="turned")
+        nc.tensor.transpose(peaks[:], dst_peaks[:, 0:1].to_broadcast([P, P]), identity[:])
+        dst = turned.tile([P, N], F32, name="dst", tag="turned")
+        for k in range(CHUNKS):
+            nc.tensor.transpose(
+                dst[:, k * P : (k + 1) * P],
+                dst_columns[:, k : k + 1].to_broadcast([P, P]),
+                identity[:],
             )
-            nc.scalar.activation(weights[n][:], w[:], ACT.Exp, bias=neg_w_max[:, n : n + 1])
+
+        u_max = held.tile([P, 1], F32, name="u_max")
+        nc.vector.reduce_max(u_max[:], peaks[:], axis=mybir.AxisListType.X)
+        neg_max = held.tile([P, 1], F32, name="neg_max")
+        nc.scalar.mul(neg_max[:], u_max[:], -1.0)
+        neg_max_slope = held.tile([P, 1], F32, name="neg_max_slope")
+        nc.scalar.mul(neg_max_slope[:], u_max[:], -SLOPE)
+        rise = held.tile([P, BLOCKS], F32, name="rise")
+        nc.vector.tensor_scalar(rise[:], src[:], u_max[:, 0:1], 0.0, op0=ALU.add, op1=ALU.max)
+        dst_listed = dst[:].rearrange("p (k q) -> p q k", k=CHUNKS)
+        plain = held.tile([P, N], F32, name="plain")
+        nc.scalar.activation(
+            plain[:].rearrange("p (q k) -> p q k", k=CHUNKS), dst_listed, ACT.Exp, bias=neg_max[:, 0:1]
+        )
+        steep = held.tile([P, BLOCKS], F32, name="steep")
+        nc.scalar.activation(steep[:], rise[:], ACT.Exp, scale=-(1.0 - SLOPE))
+        slack = held.tile([P, N], F32, name="slack")
+        nc.scalar.activation(
+            slack[:].rearrange("p (q k) -> p q k", k=CHUNKS),
+            dst_listed,
+            ACT.Exp,
+            bias=neg_max_slope[:, 0:1],
+            scale=SLOPE,
+        )
 
         sums = [summed.tile([P, D + 1], F32, name=f"sums{n}") for n in range(BLOCKS)]
+        weights = [pair.tile([P, N], F32, name=f"weight{n}", tag="weight") for n in range(BLOCKS)]
+
+        def make_weights(n):
+            nc.vector.scalar_tensor_tensor(
+                weights[n][:], slack[:], steep[:, n : n + 1], plain[:], op0=ALU.mult, op1=ALU.max
+            )
+
+        make_weights(0)
         for n in range(BLOCKS):
-            piece = P if n == BLOCKS - 1 else N
+            if n + 1 < BLOCKS:
+                make_weights(n + 1)
+            piece = {BLOCKS - 1: P, BLOCKS - 2: 2 * P}.get(n, N)
             for first in range(0, N, piece):
-                p = work.tile([P, piece], F32, name=f"p{piece}")
+                p = work.tile([P, piece], F32, name="p", tag=f"p{piece}")
                 nc.vector.tensor_tensor(
                     p[:],
                     windows[n][:].indirect(offsets[:, first // 16 : (first + piece) // 16]),
                     weights[n][:, first : first + piece],
                     ALU.mult,
                 )
-                p_turned = turned.tile([P, piece], F32, name="p_turned")
+                p_turned = turned.tile([P, piece], F32, name="p_turned", tag="turned")
                 for at in range(0, piece, P):
                     nc.tensor.transpose(p_turned[:, at : at + P], p[:, at : at + P], identity[:])
                 p_bf = work.tile([P, piece], BF16, name=f"p_bf{piece}")
@@ -91,16 +120,16 @@ def tile_graphattentionlayer_kernel(tc, adj, s_src, s_dst, hw, b, offs, out):
 
         for n in range(BLOCKS):
             z = sums[n][:, D : D + 1]
-            z_inv = work.tile([P, 1], F32, name="z_inv")
-            nc.vector.reciprocal(z_inv[:], z)
-            r_z = work.tile([P, D], F32, name="r_z")
+            scaled = work.tile([P, D + 1], F32, name="scaled", tag=f"p{P}")
+            r_z, z_inv = scaled[:, :D], scaled[:, D : D + 1]
+            nc.vector.reciprocal(z_inv, z)
             nc.vector.scalar_tensor_tensor(
-                r_z[:], bias[:], z, sums[n][:, :D], op0=ALU.mult, op1=ALU.add
+                r_z, bias[:], z, sums[n][:, :D], op0=ALU.mult, op1=ALU.add
             )
             r_exp = work.tile([P, D], F32, name="r_exp")
-            nc.scalar.activation(r_exp[:], r_z[:], ACT.Exp, scale=z_inv[:, 0:1])
+            nc.scalar.activation(r_exp[:], r_z, ACT.Exp, scale=z_inv)
             r_pos = work.tile([P, D], F32, name="r_pos")
-            nc.vector.tensor_scalar(r_pos[:], r_z[:], z_inv[:, 0:1], 0.0, op0=ALU.mult, op1=ALU.max)
+            nc.vector.tensor_scalar(r_pos[:], r_z, z_inv, 0.0, op0=ALU.mult, op1=ALU.max)
             result = work.tile([P, D], F32, name="result")
             nc.vector.scalar_tensor_tensor(
                 result[:], r_exp[:], -1.0, r_pos[:], op0=ALU.add, op1=ALU.min

@@ -36,12 +36,13 @@ def tile_graphattentionlayer_kernel(tc, adj, s_src, s_dst, hw, b, offs, out):
         windows = [held.tile([P, S], F32, name=f"window{n}") for n in range(BLOCKS)]
         for n in range(BLOCKS):
             nc.sync.dma_start(windows[n][:], adj_blocks[n])
-        bias = held.tile([P, D], F32, name="bias")
-        nc.sync.dma_start(bias[:], b.squeeze(0).partition_broadcast(P))
 
         hw_ones = held.tile([P, CHUNKS, D + PAD], BF16, name="hw_ones")
         nc.gpsimd.memset(hw_ones[:, :, D:], 1.0)
         nc.scalar.dma_start(hw_ones[:, :, :D], hw.rearrange("(k q) d -> q k d", q=P))
+
+        b_column = held.tile([P, 1], F32, name="b_column")
+        nc.scalar.dma_start(b_column[:], b.rearrange("o d -> d o"))
 
         identity = held.tile([P, P], F32, name="identity")
         make_identity(nc, identity[:])
@@ -82,6 +83,11 @@ def tile_graphattentionlayer_kernel(tc, adj, s_src, s_dst, hw, b, offs, out):
             bias=neg_max_slope[:, 0:1],
             scale=SLOPE,
         )
+
+        b_spread = turned.tile([P, D], F32, name="b_spread", tag="turned")
+        nc.tensor.transpose(b_spread[:], b_column[:, 0:1].to_broadcast([P, P]), identity[:])
+        bias = held.tile([P, D], F32, name="bias")
+        nc.scalar.copy(bias[:], b_spread[:])
 
         sums = [summed.tile([P, D + 1], F32, name=f"sums{n}") for n in range(BLOCKS)]
         weights = [pair.tile([P, N], F32, name=f"weight{n}", tag="weight") for n in range(BLOCKS)]

@@ -44,6 +44,11 @@ def tile_graphattentionlayer_kernel(tc, adj, s_src, s_dst, hw, b, offs, out):
         b_column = held.tile([P, 1], F32, name="b_column")
         nc.scalar.dma_start(b_column[:], b.rearrange("o d -> d o"))
 
+        warm = held.tile([P, 1], F32, name="warm")
+        nc.gpsimd.memset(warm[:], 0.0)
+        warm_exp = held.tile([P, 1], F32, name="warm_exp")
+        nc.scalar.activation(warm_exp[:], warm[:], ACT.Exp)
+
         identity = held.tile([P, P], F32, name="identity")
         make_identity(nc, identity[:])
 
@@ -60,14 +65,16 @@ def tile_graphattentionlayer_kernel(tc, adj, s_src, s_dst, hw, b, offs, out):
                 identity[:],
             )
 
-        u_max = held.tile([P, 1], F32, name="u_max")
-        nc.vector.reduce_max(u_max[:], peaks[:], axis=mybir.AxisListType.X)
         neg_max = held.tile([P, 1], F32, name="neg_max")
-        nc.scalar.mul(neg_max[:], u_max[:], -1.0)
+        nc.vector.tensor_reduce(
+            neg_max[:], peaks[:], axis=mybir.AxisListType.X, op=ALU.max, negate=True
+        )
         neg_max_slope = held.tile([P, 1], F32, name="neg_max_slope")
-        nc.scalar.mul(neg_max_slope[:], u_max[:], -SLOPE)
+        nc.vector.tensor_scalar_mul(neg_max_slope[:], neg_max[:], SLOPE)
         rise = held.tile([P, BLOCKS], F32, name="rise")
-        nc.vector.tensor_scalar(rise[:], src[:], u_max[:, 0:1], 0.0, op0=ALU.add, op1=ALU.max)
+        nc.vector.tensor_scalar(
+            rise[:], src[:], neg_max[:, 0:1], 0.0, op0=ALU.subtract, op1=ALU.max
+        )
         dst_listed = dst[:].rearrange("p (k q) -> p q k", k=CHUNKS)
         plain = held.tile([P, N], F32, name="plain")
         nc.scalar.activation(

import concourse.mybir as mybir
from concourse.masks import make_identity

F32, BF16, U16 = mybir.dt.float32, mybir.dt.bfloat16, mybir.dt.uint16
ALU = mybir.AluOpType
ACT = mybir.ActivationFunctionType

P = 128
C, S, N, D = 512, 2048, 512, 128
SLOPE = 0.2
BLOCKS = C // P
CHUNKS = N // P
PAD = 16

FLOPS = 2 * C * N * D


def tile_graphattentionlayer_kernel(tc, adj, s_src, s_dst, hw, b, offs, out):
    nc = tc.nc
    adj_blocks = adj.rearrange("(p n) s -> n p s", n=BLOCKS)
    out_blocks = out.rearrange("(p n) d -> n p d", n=BLOCKS)

    with (
        tc.tile_pool(name="held", bufs=1) as held,
        tc.tile_pool(name="work", bufs=4) as work,
        tc.tile_pool(name="pair", bufs=2) as pair,
        tc.psum_pool(name="turned", bufs=4) as turned,
        tc.psum_pool(name="summed", bufs=1) as summed,
    ):
        dst_columns = held.tile([P, CHUNKS], F32, name="dst_columns")
        nc.sync.dma_start(dst_columns[:], s_dst.rearrange("o (q k) -> q (k o)", k=CHUNKS))
        src = held.tile([P, BLOCKS], F32, name="src")
        nc.sync.dma_start(src[:], s_src.rearrange("(p n) o -> p (n o)", n=BLOCKS))
        offsets = held.tile([P, N // 16], U16, name="offsets")
        nc.sync.dma_start(offsets[:], offs)
        windows = [held.tile([P, S], F32, name=f"window{n}") for n in range(BLOCKS)]
        for n in range(BLOCKS):
            nc.sync.dma_start(windows[n][:], adj_blocks[n])

        hw_ones = held.tile([P, CHUNKS, D + PAD], BF16, name="hw_ones")
        nc.gpsimd.memset(hw_ones[:, :, D:], 1.0)
        nc.scalar.dma_start(hw_ones[:, :, :D], hw.rearrange("(k q) d -> q k d", q=P))

        b_column = held.tile([P, 1], F32, name="b_column")
        nc.scalar.dma_start(b_column[:], b.rearrange("o d -> d o"))

        warm = held.tile([P, 1], F32, name="warm")
        nc.gpsimd.memset(warm[:], 0.0)
        warm_exp = held.tile([P, 1], F32, name="warm_exp")
        nc.scalar.activation(warm_exp[:], warm[:], ACT.Exp)

        identity = held.tile([P, P], F32, name="identity")
        make_identity(nc, identity[:])

        dst_peaks = held.tile([P, 1], F32, name="dst_peaks")
        nc.vector.reduce_max(dst_peaks[:], dst_columns[:], axis=mybir.AxisListType.X)

        peaks = turned.tile([P, P], F32, name="peaks", tag="turned")
        nc.tensor.transpose(peaks[:], dst_peaks[:, 0:1].to_broadcast([P, P]), identity[:])
        dst = turned.tile([P, N], F32, name="dst", tag="turned")
        for k in range(CHUNKS):
            nc.tensor.transpose(
                dst[:, k * P : (k + 1) * P],
                dst_columns[:, k : k + 1].to_broadcast([P, P]),
                identity[:],
            )

        neg_max = held.tile([P, 1], F32, name="neg_max")
        nc.vector.tensor_reduce(
            neg_max[:], peaks[:], axis=mybir.AxisListType.X, op=ALU.max, negate=True
        )
        neg_max_slope = held.tile([P, 1], F32, name="neg_max_slope")
        nc.vector.tensor_scalar_mul(neg_max_slope[:], neg_max[:], SLOPE)
        rise = held.tile([P, BLOCKS], F32, name="rise")
        nc.vector.tensor_scalar(
            rise[:], src[:], neg_max[:, 0:1], 0.0, op0=ALU.subtract, op1=ALU.max
        )
        dst_listed = dst[:].rearrange("p (k q) -> p q k", k=CHUNKS)
        plain = held.tile([P, N], F32, name="plain")
        nc.scalar.activation(
            plain[:].rearrange("p (q k) -> p q k", k=CHUNKS), dst_listed, ACT.Exp, bias=neg_max[:, 0:1]
        )
        steep = held.tile([P, BLOCKS], F32, name="steep")
        nc.scalar.activation(steep[:], rise[:], ACT.Exp, scale=-(1.0 - SLOPE))
        slack = held.tile([P, N], F32, name="slack")
        nc.scalar.activation(
            slack[:].rearrange("p (q k) -> p q k", k=CHUNKS),
            dst_listed,
            ACT.Exp,
            bias=neg_max_slope[:, 0:1],
            scale=SLOPE,
        )

        b_spread = turned.tile([P, D], F32, name="b_spread", tag="turned")
        nc.tensor.transpose(b_spread[:], b_column[:, 0:1].to_broadcast([P, P]), identity[:])
        bias = held.tile([P, D], F32, name="bias")
        nc.scalar.copy(bias[:], b_spread[:])

        sums = [summed.tile([P, D + 1], F32, name=f"sums{n}") for n in range(BLOCKS)]
        weights = [pair.tile([P, N], F32, name=f"weight{n}", tag="weight") for n in range(BLOCKS)]

        def make_weights(n):
            nc.vector.scalar_tensor_tensor(
                weights[n][:], slack[:], steep[:, n : n + 1], plain[:], op0=ALU.mult, op1=ALU.max
            )

        make_weights(0)
        for n in range(BLOCKS):
            if n + 1 < BLOCKS:
                make_weights(n + 1)
            piece = {BLOCKS - 1: P, BLOCKS - 2: 2 * P}.get(n, N)
            for first in range(0, N, piece):
                p = work.tile([P, piece], F32, name="p", tag=f"p{piece}")
                nc.vector.tensor_tensor(
                    p[:],
                    windows[n][:].indirect(offsets[:, first // 16 : (first + piece) // 16]),
                    weights[n][:, first : first + piece],
                    ALU.mult,
                )
                p_turned = turned.tile([P, piece], F32, name="p_turned", tag="turned")
                for at in range(0, piece, P):
                    nc.tensor.transpose(p_turned[:, at : at + P], p[:, at : at + P], identity[:])
                p_bf = work.tile([P, piece], BF16, name=f"p_bf{piece}")
                nc.scalar.copy(p_bf[:], p_turned[:])
                for at in range(0, piece, P):
                    nc.tensor.matmul(
                        sums[n][:],
                        lhsT=p_bf[:, at : at + P],
                        rhs=hw_ones[:, (first + at) // P, : D + 1],
                        start=(first + at == 0),
                        stop=(first + at == N - P),
                    )

        for n in range(BLOCKS):
            z = sums[n][:, D : D + 1]
            scaled = work.tile([P, D + 1], F32, name="scaled", tag=f"p{P}")
            r_z, z_inv = scaled[:, :D], scaled[:, D : D + 1]
            nc.vector.reciprocal(z_inv, z)
            nc.vector.scalar_tensor_tensor(
                r_z, bias[:], z, sums[n][:, :D], op0=ALU.mult, op1=ALU.add
            )
            r_exp = work.tile([P, D], F32, name="r_exp")
            nc.scalar.activation(r_exp[:], r_z, ACT.Exp, scale=z_inv)
            r_pos = work.tile([P, D], F32, name="r_pos")
            nc.vector.tensor_scalar(r_pos[:], r_z, z_inv, 0.0, op0=ALU.mult, op1=ALU.max)
            result = work.tile([P, D], F32, name="result")
            nc.vector.scalar_tensor_tensor(
                result[:], r_exp[:], -1.0, r_pos[:], op0=ALU.add, op1=ALU.min
            )
            nc.sync.dma_start(out_blocks[n], result[:])
